import numpy as np
import ml_dtypes


def mxq(x, axis, fmt="e4m3"):
    dtype, down = {"e4m3": (ml_dtypes.float8_e4m3fn, 7), "e5m2": (ml_dtypes.float8_e5m2, 14)}[fmt]
    v = np.moveaxis(np.asarray(x, np.float32).astype(ml_dtypes.bfloat16).astype(np.float64), axis, -1)
    blocks = v.reshape(v.shape[:-1] + (-1, 32))
    amax = np.abs(blocks).max(-1, keepdims=True)
    byte = np.maximum(np.where(amax > 0, np.frexp(amax)[1] - 1 + 127, 0) - down, 1)
    scale = np.exp2(byte - 127.0)
    codes = (blocks / scale).astype(np.float32).astype(dtype).astype(np.float64)
    return np.moveaxis((codes * scale).reshape(v.shape), -1, axis)


WIDE = False


def mx_kscale(k):
    if not WIDE:
        return np.ones(k)
    levels = np.array([10, -10, 5, -5, 0])
    a = np.random.permutation(np.resize(levels, k // 512 * 4)).reshape(k // 512, 4)
    idx = np.arange(k)
    return np.exp2(a[idx // 512, idx % 128 // 32])


BF16 = ml_dtypes.bfloat16


def bf(x):
    return np.asarray(x, np.float32).astype(BF16)


def f64(x):
    return np.asarray(x).astype(np.float64)


E2M1 = np.array([0.0, 0.5, 1.0, 1.5, 2.0, 3.0, 4.0, 6.0, -0.0, -0.5, -1.0, -1.5, -2.0, -3.0, -4.0, -6.0])


def pack_weight(w, fmt):
    k, n = w.shape
    w = f64(bf(w)).reshape(k // 32, 32, n)
    amax = np.abs(w).max(1)
    if fmt == "e4m3":
        byte = np.frexp(amax)[1] - 1 + 127 - 7
    else:
        mant, ex = np.frexp(amax / 6.0)
        byte = np.where(mant > 0.5, ex, ex - 1) + 127
    byte = np.clip(np.where(amax > 0, byte, 1), 1, 254)
    scaled = (w * np.exp2(127.0 - byte)[:, None, :]).reshape(k, n).astype(np.float32)
    by_word = np.ascontiguousarray(scaled.reshape(k // 512, 128, 4, n).transpose(0, 1, 3, 2))
    if fmt == "e4m3":
        words = by_word.astype(ml_dtypes.float8_e4m3fn).view(np.uint8)
    else:
        c = by_word.astype(ml_dtypes.float4_e2m1fn).view(np.uint8) & 0xF
        words = c[..., 0::2] | (c[..., 1::2] << 4)
    return np.ascontiguousarray(words), np.ascontiguousarray(byte.astype(np.uint8).reshape(k // 512, 16, n))


def unpack_weight(words, scales, fmt):
    g, p, n, _ = words.shape
    if fmt == "e4m3":
        vals = np.ascontiguousarray(words).view(ml_dtypes.float8_e4m3fn).astype(np.float64)
    else:
        nib = np.empty((g, p, n, 4), np.uint8)
        nib[..., 0::2] = words & 0xF
        nib[..., 1::2] = words >> 4
        vals = E2M1[nib]
    vals = vals * np.repeat(np.exp2(scales.astype(np.float64) - 127.0), 8, axis=1)[..., None]
    return vals.transpose(0, 1, 3, 2).reshape(g * 512, n)


B, S, E, H, KV, DH = 1, 128, 8192, 16, 4, 128
THETA = 10000.0
FMT = "e4m3"


def rope(x):
    b, s, h, hd = x.shape
    half = hd // 2
    inv_freq = 1.0 / THETA ** (f64(np.arange(0, half, 2)) / half)
    pos = np.broadcast_to(f64(np.arange(s))[None, :], (b, s))
    freqs = pos[:, :, None] * inv_freq[None, None, :]
    cos = np.cos(freqs)[:, :, None, :]
    sin = np.sin(freqs)[:, :, None, :]
    pairs = x[..., :half].reshape(b, s, h, half // 2, 2)
    x0, x1 = pairs[..., 0], pairs[..., 1]
    rot = np.stack([x0 * cos - x1 * sin, x0 * sin + x1 * cos], axis=-1).reshape(b, s, h, half)
    return np.concatenate([rot, x[..., half:]], axis=-1)


def setup_inputs():
    s = mx_kscale(E)
    hidden_states = bf(np.random.standard_normal((B, S, E)) * s)
    wq_words, wq_scales = pack_weight(np.random.standard_normal((E, H * DH)) * 1.25 / np.sqrt(E) / s[:, None], FMT)
    wk_words, wk_scales = pack_weight(np.random.standard_normal((E, KV * DH)) * 1.25 / np.sqrt(E) / s[:, None], FMT)
    wv_words, wv_scales = pack_weight(np.random.standard_normal((E, KV * DH)) * 1.25 / np.sqrt(E) / s[:, None], FMT)
    return {"hidden_states": hidden_states,
            "Wq_words": wq_words, "Wq_scales": wq_scales,
            "Wk_words": wk_words, "Wk_scales": wk_scales,
            "Wv_words": wv_words, "Wv_scales": wv_scales}


def reference(hidden_states, Wq_words, Wq_scales, Wk_words, Wk_scales, Wv_words, Wv_scales):
    xq = mxq(f64(hidden_states), 2, "e4m3")
    q = (xq @ unpack_weight(Wq_words, Wq_scales, FMT)).reshape(B, S, H, DH)
    k = (xq @ unpack_weight(Wk_words, Wk_scales, FMT)).reshape(B, S, KV, DH)
    v = (xq @ unpack_weight(Wv_words, Wv_scales, FMT)).reshape(B, S, KV, DH)
    return rope(q), rope(k), v

@@ -1,0 +1,229 @@
+import math
+from contextlib import ExitStack
+
+import concourse.mybir as mybir
+from concourse.masks import make_identity
+
+F32 = mybir.dt.float32
+BF16 = mybir.dt.bfloat16
+I32 = mybir.dt.int32
+U32 = mybir.dt.uint32
+U8 = mybir.dt.uint8
+FP8X4 = mybir.dt.float8_e4m3fn_x4
+SIN = mybir.ActivationFunctionType.Sin
+
+P = 128
+E = 8192
+K_PASS = 512
+PASSES = E // K_PASS
+N_TILE = 512
+HEAD = 128
+ROTATED = 64
+PAIRS = ROTATED // 2
+THETA = 10000.0
+Q_COLS = 2048
+KV_COLS = 512
+
+LANES = 4
+SLOTS = PASSES // LANES
+
+X_CHUNK_PASSES = 4
+BANK_PASSES = 2
+KV_CHUNK_PASSES = 4
+WEIGHT_BUFS = 16
+
+ROUND_MAGIC = 1.5 * 2.0**23
+
+FLOPS = 2 * P * E * (Q_COLS + 2 * KV_COLS)
+
+
+def load_scale_planes(nc, planes, scales):
+    for slot in range(SLOTS):
+        for quadrant in range(4):
+            nc.gpsimd.dma_start(
+                out=planes[32 * quadrant : 32 * quadrant + 4 * LANES, slot, :].bitcast(F32),
+                in_=scales[
+                    LANES * slot : LANES * (slot + 1), 4 * quadrant : 4 * quadrant + 4, :
+                ].bitcast(F32),
+            )
+
+
+def add_pass(nc, acc, x_codes, x_scales, g, words, planes, cols):
+    nc.tensor.matmul_mx(
+        out=acc[:],
+        lhsT=x_codes[:, g, :].bitcast(FP8X4),
+        lhsT_scale=x_scales[:, g, :],
+        rhs=words.bitcast(FP8X4),
+        rhs_scale=planes[4 * (g % LANES) : P, g // LANES, cols],
+        start=(g == 0),
+        stop=(g == PASSES - 1),
+    )
+
+
+def rotate_pairs(nc, work, rows, heads, sin, cos):
+    pairs = rows.rearrange("p (h f) -> p h f", f=HEAD)[:, :, 0:ROTATED].rearrange(
+        "p h (i e) -> p h i e", e=2
+    )
+    even = pairs[:, :, :, 0]
+    odd = pairs[:, :, :, 1]
+    sin_all = sin.unsqueeze(1).to_broadcast([P, heads, PAIRS])
+    cos_all = cos.unsqueeze(1).to_broadcast([P, heads, PAIRS])
+    even_cos = work.tile([P, heads, PAIRS], F32)
+    odd_sin = work.tile([P, heads, PAIRS], F32)
+    even_sin = work.tile([P, heads, PAIRS], F32)
+    odd_cos = work.tile([P, heads, PAIRS], F32)
+    nc.vector.tensor_mul(out=even_cos[:], in0=even, in1=cos_all)
+    nc.vector.tensor_mul(out=odd_sin[:], in0=odd, in1=sin_all)
+    nc.vector.tensor_mul(out=even_sin[:], in0=even, in1=sin_all)
+    nc.vector.tensor_mul(out=odd_cos[:], in0=odd, in1=cos_all)
+    nc.vector.tensor_sub(out=even, in0=even_cos[:], in1=odd_sin[:])
+    nc.vector.tensor_add(out=odd, in0=even_sin[:], in1=odd_cos[:])
+
+
+def tile_diffucoderattention_pa_k_kernel(
+    tc,
+    hidden_states,
+    Wq_words,
+    Wq_scales,
+    Wk_words,
+    Wk_scales,
+    Wv_words,
+    Wv_scales,
+    out_0,
+    out_1,
+    out_2,
+):
+    nc = tc.nc
+    x_dram = hidden_states.rearrange("b s e -> (b s) e")
+
+    with ExitStack() as ctx:
+        keep = ctx.enter_context(tc.tile_pool(name="keep", bufs=1))
+        x_pool = ctx.enter_context(tc.tile_pool(name="x_pool", bufs=PASSES // X_CHUNK_PASSES))
+        stage = ctx.enter_context(tc.tile_pool(name="stage", bufs=3))
+        weights = ctx.enter_context(tc.tile_pool(name="weights", bufs=WEIGHT_BUFS))
+        work = ctx.enter_context(tc.tile_pool(name="work", bufs=1))
+        sums = ctx.enter_context(tc.psum_pool(name="sums", bufs=1))
+        flipped = ctx.enter_context(tc.psum_pool(name="flipped", bufs=2))
+
+        q_planes = keep.tile([P, SLOTS, Q_COLS], U8, align_bytes=64)
+        k_planes = keep.tile([P, SLOTS, KV_COLS], U8, align_bytes=64)
+        v_planes = keep.tile([P, SLOTS, KV_COLS], U8, align_bytes=64)
+        for planes in (q_planes, k_planes, v_planes):
+            nc.vector.memset(planes[:].rearrange("p s n -> p (s n)").bitcast(I32), 0)
+
+        identity = keep.tile([P, P], F32)
+        make_identity(nc, identity[:])
+        position_int = keep.tile([P, 1], I32)
+        nc.gpsimd.iota(position_int[:], pattern=[[0, 1]], base=0, channel_multiplier=1)
+
+        x_chunks = []
+        for c in range(PASSES // X_CHUNK_PASSES):
+            x_chunk = x_pool.tile([P, X_CHUNK_PASSES * K_PASS], BF16)
+            nc.sync.dma_start(
+                out=x_chunk[:],
+                in_=x_dram[:, c * X_CHUNK_PASSES * K_PASS : (c + 1) * X_CHUNK_PASSES * K_PASS],
+            )
+            x_chunks.append(x_chunk)
+
+        load_scale_planes(nc, q_planes, Wq_scales)
+        load_scale_planes(nc, k_planes, Wk_scales)
+        load_scale_planes(nc, v_planes, Wv_scales)
+
+        x_codes = keep.tile([P, PASSES, P], U32, align_bytes=64)
+        x_scales = keep.tile([P, PASSES, P], U8, align_bytes=64)
+        words_a_pass = K_PASS // 2
+        for bank in range(PASSES // BANK_PASSES):
+            first = bank * BANK_PASSES
+            x_words = x_chunks[first // X_CHUNK_PASSES][:].bitcast(F32)
+            turned = flipped.tile([P, BANK_PASSES, 2, P], F32)
+            for i in range(BANK_PASSES):
+                start_word = ((first + i) % X_CHUNK_PASSES) * words_a_pass
+                for u in range(2):
+                    nc.tensor.transpose(
+                        turned[:, i, u, :],
+                        x_words[:, start_word + u : start_word + words_a_pass : 2],
+                        identity[:],
+                    )
+            grouped = stage.tile([P, BANK_PASSES * P * 4], BF16, align_bytes=64)
+            grouped_words = grouped[:].bitcast(F32).rearrange(
+                "p (i r u) -> p i r u", i=BANK_PASSES, u=2
+            )
+            if bank % 2 == 0:
+                nc.vector.tensor_copy(out=grouped_words, in_=turned[:].rearrange("p i u r -> p i r u"))
+            else:
+                nc.scalar.copy(out=grouped_words, in_=turned[:].rearrange("p i u r -> p i r u"))
+            nc.vector.quantize_mx(
+                out=x_codes[:, first : first + BANK_PASSES, :]
+                .rearrange("p i r -> p (i r)")
+                .bitcast(FP8X4),
+                scales=x_scales[:, first : first + BANK_PASSES, :].rearrange("p i r -> p (i r)"),
+                in_=grouped[:],
+            )
+
+        position = keep.tile([P, 1], F32)
+        nc.vector.tensor_copy(out=position[:], in_=position_int[:])
+        phase = keep.tile([P, 2, PAIRS], F32)
+        nc.vector.tensor_scalar_mul(out=phase[:, 0, 0:1], in0=position[:], scalar1=0.5 / math.pi)
+        ratio = THETA ** (-2.0 / ROTATED)
+        width = 1
+        while width < PAIRS:
+            nc.vector.tensor_scalar_mul(
+                out=phase[:, 0, width : 2 * width], in0=phase[:, 0, 0:width], scalar1=ratio**width
+            )
+            width *= 2
+        nc.vector.tensor_scalar_add(out=phase[:, 1, :], in0=phase[:, 0, :], scalar1=0.25)
+        shifted = keep.tile([P, 2, PAIRS], F32)
+        nc.vector.tensor_scalar_add(out=shifted[:], in0=phase[:], scalar1=ROUND_MAGIC)
+        whole = keep.tile([P, 2, PAIRS], F32)
+        nc.vector.tensor_scalar_sub(out=whole[:], in0=shifted[:], scalar1=ROUND_MAGIC)
+        part = keep.tile([P, 2, PAIRS], F32)
+        nc.vector.tensor_sub(out=part[:], in0=phase[:], in1=whole[:])
+        sin_cos = keep.tile([P, 2, PAIRS], F32)
+        nc.scalar.activation(out=sin_cos[:], in_=part[:], func=SIN, scale=2.0 * math.pi)
+        sin = sin_cos[:, 0, :]
+        cos = sin_cos[:, 1, :]
+
+        q_tiles = Q_COLS // N_TILE
+        q_sums = [sums.tile([P, N_TILE], F32, name="q_sum%d" % j) for j in range(q_tiles)]
+        for g in range(PASSES):
+            q_words = weights.tile([P, Q_COLS], U32, tag="weights", align_bytes=64)
+            nc.sync.dma_start(
+                out=q_words[:].bitcast(I32),
+                in_=Wq_words[g].rearrange("p n t -> p (n t)").bitcast(I32),
+            )
+            for j in range(q_tiles):
+                cols = slice(j * N_TILE, (j + 1) * N_TILE)
+                add_pass(nc, q_sums[j], x_codes, x_scales, g, q_words[:, cols], q_planes, cols)
+
+        q_rows = keep.tile([P, Q_COLS], F32)
+        for j in range(q_tiles):
+            cols = slice(j * N_TILE, (j + 1) * N_TILE)
+            if j % 2 == 0:
+                nc.vector.tensor_copy(out=q_rows[:, cols], in_=q_sums[j][:])
+            else:
+                nc.scalar.copy(out=q_rows[:, cols], in_=q_sums[j][:])
+        rotate_pairs(nc, work, q_rows[:], Q_COLS // HEAD, sin, cos)
+        nc.sync.dma_start(out=out_0.rearrange("b s h d -> (b s) (h d)"), in_=q_rows[:])
+
+        all_cols = slice(0, KV_COLS)
+        for name, w_dram, planes, out in (
+            ("k", Wk_words, k_planes, out_1),
+            ("v", Wv_words, v_planes, out_2),
+        ):
+            kv_sum = sums.tile([P, KV_COLS], F32, name=name + "_sum")
+            for c in range(PASSES // KV_CHUNK_PASSES):
+                kv_words = weights.tile([P, KV_CHUNK_PASSES, KV_COLS], U32, tag="weights", align_bytes=64)
+                nc.sync.dma_start(
+                    out=kv_words[:].bitcast(I32),
+                    in_=w_dram[c * KV_CHUNK_PASSES : (c + 1) * KV_CHUNK_PASSES]
+                    .rearrange("g p n t -> p g (n t)")
+                    .bitcast(I32),
+                )
+                for i in range(KV_CHUNK_PASSES):
+                    g = c * KV_CHUNK_PASSES + i
+                    add_pass(nc, kv_sum, x_codes, x_scales, g, kv_words[:, i, :], planes, all_cols)
+            kv_rows = keep.tile([P, KV_COLS], F32, name=name + "_rows")
+            nc.scalar.copy(out=kv_rows[:], in_=kv_sum[:])
+            if name == "k":
+                rotate_pairs(nc, work, kv_rows[:], KV_COLS // HEAD, sin, cos)
+            nc.sync.dma_start(out=out.rearrange("b s h d -> (b s) (h d)"), in_=kv_rows[:])

@@ -37,15 +37,19 @@ ROUND_MAGIC = 1.5 * 2.0**23
 FLOPS = 2 * P * E * (Q_COLS + 2 * KV_COLS)
 
 
+def load_scale_rows(queue, word, planes, scales, slot, quadrant):
+    queue.dma_start(
+        out=planes[32 * quadrant : 32 * quadrant + 4 * LANES, slot, :].bitcast(word),
+        in_=scales[
+            LANES * slot : LANES * (slot + 1), 4 * quadrant : 4 * quadrant + 4, :
+        ].bitcast(word),
+    )
+
+
 def load_scale_planes(nc, planes, scales):
     for slot in range(SLOTS):
         for quadrant in range(4):
-            nc.gpsimd.dma_start(
-                out=planes[32 * quadrant : 32 * quadrant + 4 * LANES, slot, :].bitcast(F32),
-                in_=scales[
-                    LANES * slot : LANES * (slot + 1), 4 * quadrant : 4 * quadrant + 4, :
-                ].bitcast(F32),
-            )
+            load_scale_rows(nc.gpsimd, F32, planes, scales, slot, quadrant)
 
 
 def add_pass(nc, acc, x_codes, x_scales, g, words, planes, cols):
@@ -127,7 +131,6 @@ def tile_diffucoderattention_pa_k_kernel(
 
         load_scale_planes(nc, q_planes, Wq_scales)
         load_scale_planes(nc, k_planes, Wk_scales)
-        load_scale_planes(nc, v_planes, Wv_scales)
 
         x_codes = keep.tile([P, PASSES, P], U32, align_bytes=64)
         x_scales = keep.tile([P, PASSES, P], U8, align_bytes=64)
@@ -191,6 +194,7 @@ def tile_diffucoderattention_pa_k_kernel(
                 out=q_words[:].bitcast(I32),
                 in_=Wq_words[g].rearrange("p n t -> p (n t)").bitcast(I32),
             )
+            load_scale_rows(nc.sync, I32, v_planes, Wv_scales, g // 4, g % 4)
             for j in range(q_tiles):
                 cols = slice(j * N_TILE, (j + 1) * N_TILE)
                 add_pass(nc, q_sums[j], x_codes, x_scales, g, q_words[:, cols], q_planes, cols)

@@ -207,7 +207,7 @@ def tile_diffucoderattention_pa_k_kernel(
             else:
                 nc.scalar.copy(out=q_rows[:, cols], in_=q_sums[j][:])
         rotate_pairs(nc, work, q_rows[:], Q_COLS // HEAD, sin, cos)
-        nc.sync.dma_start(out=out_0.rearrange("b s h d -> (b s) (h d)"), in_=q_rows[:])
+        nc.scalar.dma_start(out=out_0.rearrange("b s h d -> (b s) (h d)"), in_=q_rows[:])
 
         all_cols = slice(0, KV_COLS)
         for name, w_dram, planes, out in (
@@ -230,4 +230,4 @@ def tile_diffucoderattention_pa_k_kernel(
             nc.scalar.copy(out=kv_rows[:], in_=kv_sum[:])
             if name == "k":
                 rotate_pairs(nc, work, kv_rows[:], KV_COLS // HEAD, sin, cos)
-            nc.sync.dma_start(out=out.rearrange("b s h d -> (b s) (h d)"), in_=kv_rows[:])
+            nc.scalar.dma_start(out=out.rearrange("b s h d -> (b s) (h d)"), in_=kv_rows[:])

@@ -29,7 +29,8 @@ SLOTS = PASSES // LANES
 
 X_CHUNK_PASSES = 4
 BANK_PASSES = 2
-KV_CHUNK_PASSES = 4
+K_CHUNKS = (4, 4, 4, 4)
+V_CHUNKS = (4, 4, 4, 3, 1)
 WEIGHT_BUFS = 16
 
 ROUND_MAGIC = 1.5 * 2.0**23
@@ -62,6 +63,20 @@ def add_pass(nc, acc, x_codes, x_scales, g, words, planes, cols):
         start=(g == 0),
         stop=(g == PASSES - 1),
     )
+
+
+def kv_passes(nc, weights, w_dram, chunks):
+    passes = []
+    first = 0
+    for count in chunks:
+        chunk = weights.tile([P, max(chunks), KV_COLS], U32, tag="weights", align_bytes=64)
+        nc.sync.dma_start(
+            out=chunk[:, 0:count, :].bitcast(I32),
+            in_=w_dram[first : first + count].rearrange("g p n t -> p g (n t)").bitcast(I32),
+        )
+        passes.extend((first + i, chunk[:, i, :]) for i in range(count))
+        first += count
+    return passes
 
 
 def rotate_pairs(nc, work, rows, heads, sin, cos):
@@ -131,6 +146,7 @@ def tile_diffucoderattention_pa_k_kernel(
 
         load_scale_planes(nc, q_planes, Wq_scales)
         load_scale_planes(nc, k_planes, Wk_scales)
+        load_scale_planes(nc, v_planes, Wv_scales)
 
         x_codes = keep.tile([P, PASSES, P], U32, align_bytes=64)
         x_scales = keep.tile([P, PASSES, P], U8, align_bytes=64)
@@ -194,7 +210,6 @@ def tile_diffucoderattention_pa_k_kernel(
                 out=q_words[:].bitcast(I32),
                 in_=Wq_words[g].rearrange("p n t -> p (n t)").bitcast(I32),
             )
-            load_scale_rows(nc.sync, I32, v_planes, Wv_scales, g // 4, g % 4)
             for j in range(q_tiles):
                 cols = slice(j * N_TILE, (j + 1) * N_TILE)
                 add_pass(nc, q_sums[j], x_codes, x_scales, g, q_words[:, cols], q_planes, cols)
@@ -209,25 +224,23 @@ def tile_diffucoderattention_pa_k_kernel(
         rotate_pairs(nc, work, q_rows[:], Q_COLS // HEAD, sin, cos)
         nc.scalar.dma_start(out=out_0.rearrange("b s h d -> (b s) (h d)"), in_=q_rows[:])
 
-        all_cols = slice(0, KV_COLS)
-        for name, w_dram, planes, out in (
-            ("k", Wk_words, k_planes, out_1),
-            ("v", Wv_words, v_planes, out_2),
-        ):
-            kv_sum = sums.tile([P, KV_COLS], F32, name=name + "_sum")
-            for c in range(PASSES // KV_CHUNK_PASSES):
-                kv_words = weights.tile([P, KV_CHUNK_PASSES, KV_COLS], U32, tag="weights", align_bytes=64)
-                nc.sync.dma_start(
-                    out=kv_words[:].bitcast(I32),
-                    in_=w_dram[c * KV_CHUNK_PASSES : (c + 1) * KV_CHUNK_PASSES]
-                    .rearrange("g p n t -> p g (n t)")
-                    .bitcast(I32),
-                )
-                for i in range(KV_CHUNK_PASSES):
-                    g = c * KV_CHUNK_PASSES + i
-                    add_pass(nc, kv_sum, x_codes, x_scales, g, kv_words[:, i, :], planes, all_cols)
-            kv_rows = keep.tile([P, KV_COLS], F32, name=name + "_rows")
-            nc.scalar.copy(out=kv_rows[:], in_=kv_sum[:])
-            if name == "k":
-                rotate_pairs(nc, work, kv_rows[:], KV_COLS // HEAD, sin, cos)
-            nc.scalar.dma_start(out=out.rearrange("b s h d -> (b s) (h d)"), in_=kv_rows[:])
+        k_sum = sums.tile([P, KV_COLS], F32, name="k_sum")
+        for g, words in kv_passes(nc, weights, Wk_words, K_CHUNKS):
+            add_pass(nc, k_sum, x_codes, x_scales, g, words, k_planes, slice(0, KV_COLS))
+        k_rows = keep.tile([P, KV_COLS], F32)
+        nc.scalar.copy(out=k_rows[:], in_=k_sum[:])
+        rotate_pairs(nc, work, k_rows[:], KV_COLS // HEAD, sin, cos)
+        nc.scalar.dma_start(out=out_1.rearrange("b s h d -> (b s) (h d)"), in_=k_rows[:])
+
+        v_out = out_2.rearrange("b s h d -> (b s) (h d)")
+        halves = (slice(0, KV_COLS // 2), slice(KV_COLS // 2, KV_COLS))
+        v_sums = [flipped.tile([P, KV_COLS // 2], F32, name="v_sum%d" % j, tag="turned") for j in range(2)]
+        for g, words in kv_passes(nc, weights, Wv_words, V_CHUNKS):
+            for v_sum, cols in zip(v_sums, halves):
+                add_pass(nc, v_sum, x_codes, x_scales, g, words[:, cols], v_planes, cols)
+        v_left = keep.tile([P, KV_COLS // 2], F32)
+        v_right = keep.tile([P, KV_COLS // 2], F32)
+        nc.vector.tensor_copy(out=v_left[:], in_=v_sums[0][:])
+        nc.scalar.copy(out=v_right[:], in_=v_sums[1][:])
+        nc.sync.dma_start(out=v_out[:, halves[0]], in_=v_left[:])
+        nc.scalar.dma_start(out=v_out[:, halves[1]], in_=v_right[:])

@@ -47,9 +47,9 @@ def load_scale_rows(queue, word, planes, scales, slot, quadrant):
     )
 
 
-def load_scale_planes(nc, planes, scales):
+def load_upper_scales(nc, planes, scales):
     for slot in range(SLOTS):
-        for quadrant in range(4):
+        for quadrant in (2, 3):
             load_scale_rows(nc.gpsimd, F32, planes, scales, slot, quadrant)
 
 
@@ -144,9 +144,12 @@ def tile_diffucoderattention_pa_k_kernel(
             )
             x_chunks.append(x_chunk)
 
-        load_scale_planes(nc, q_planes, Wq_scales)
-        load_scale_planes(nc, k_planes, Wk_scales)
-        load_scale_planes(nc, v_planes, Wv_scales)
+        for slot in range(SLOTS):
+            for quadrant in (0, 1):
+                load_scale_rows(nc.sync, I32, q_planes, Wq_scales, slot, quadrant)
+        load_upper_scales(nc, q_planes, Wq_scales)
+        load_upper_scales(nc, k_planes, Wk_scales)
+        load_upper_scales(nc, v_planes, Wv_scales)
 
         x_codes = keep.tile([P, PASSES, P], U32, align_bytes=64)
         x_scales = keep.tile([P, PASSES, P], U8, align_bytes=64)
@@ -210,6 +213,8 @@ def tile_diffucoderattention_pa_k_kernel(
                 out=q_words[:].bitcast(I32),
                 in_=Wq_words[g].rearrange("p n t -> p (n t)").bitcast(I32),
             )
+            planes, scales = ((k_planes, Wk_scales), (v_planes, Wv_scales))[g // 8]
+            load_scale_rows(nc.sync, I32, planes, scales, (g % 8) // 2, g % 2)
             for j in range(q_tiles):
                 cols = slice(j * N_TILE, (j + 1) * N_TILE)
                 add_pass(nc, q_sums[j], x_codes, x_scales, g, q_words[:, cols], q_planes, cols)

import math
from contextlib import ExitStack

import concourse.mybir as mybir
from concourse.masks import make_identity

F32 = mybir.dt.float32
BF16 = mybir.dt.bfloat16
I32 = mybir.dt.int32
U32 = mybir.dt.uint32
U8 = mybir.dt.uint8
FP8X4 = mybir.dt.float8_e4m3fn_x4
SIN = mybir.ActivationFunctionType.Sin

P = 128
E = 8192
K_PASS = 512
PASSES = E // K_PASS
N_TILE = 512
HEAD = 128
ROTATED = 64
PAIRS = ROTATED // 2
THETA = 10000.0
Q_COLS = 2048
KV_COLS = 512

LANES = 4
SLOTS = PASSES // LANES

X_CHUNK_PASSES = 4
BANK_PASSES = 2
K_CHUNKS = (4, 4, 4, 4)
V_CHUNKS = (4, 4, 4, 3, 1)
WEIGHT_BUFS = 16

ROUND_MAGIC = 1.5 * 2.0**23

FLOPS = 2 * P * E * (Q_COLS + 2 * KV_COLS)


def load_scale_rows(queue, word, planes, scales, slot, quadrant):
    queue.dma_start(
        out=planes[32 * quadrant : 32 * quadrant + 4 * LANES, slot, :].bitcast(word),
        in_=scales[
            LANES * slot : LANES * (slot + 1), 4 * quadrant : 4 * quadrant + 4, :
        ].bitcast(word),
    )


def load_upper_scales(nc, planes, scales):
    for slot in range(SLOTS):
        for quadrant in (2, 3):
            load_scale_rows(nc.gpsimd, F32, planes, scales, slot, quadrant)


def add_pass(nc, acc, x_codes, x_scales, g, words, planes, cols):
    nc.tensor.matmul_mx(
        out=acc[:],
        lhsT=x_codes[:, g, :].bitcast(FP8X4),
        lhsT_scale=x_scales[:, g, :],
        rhs=words.bitcast(FP8X4),
        rhs_scale=planes[4 * (g % LANES) : P, g // LANES, cols],
        start=(g == 0),
        stop=(g == PASSES - 1),
    )


def kv_passes(nc, weights, w_dram, chunks):
    passes = []
    first = 0
    for count in chunks:
        chunk = weights.tile([P, max(chunks), KV_COLS], U32, tag="weights", align_bytes=64)
        nc.sync.dma_start(
            out=chunk[:, 0:count, :].bitcast(I32),
            in_=w_dram[first : first + count].rearrange("g p n t -> p g (n t)").bitcast(I32),
        )
        passes.extend((first + i, chunk[:, i, :]) for i in range(count))
        first += count
    return passes


def rotate_pairs(nc, work, rows, heads, sin, cos):
    pairs = rows.rearrange("p (h f) -> p h f", f=HEAD)[:, :, 0:ROTATED].rearrange(
        "p h (i e) -> p h i e", e=2
    )
    even = pairs[:, :, :, 0]
    odd = pairs[:, :, :, 1]
    sin_all = sin.unsqueeze(1).to_broadcast([P, heads, PAIRS])
    cos_all = cos.unsqueeze(1).to_broadcast([P, heads, PAIRS])
    even_cos = work.tile([P, heads, PAIRS], F32)
    odd_sin = work.tile([P, heads, PAIRS], F32)
    even_sin = work.tile([P, heads, PAIRS], F32)
    odd_cos = work.tile([P, heads, PAIRS], F32)
    nc.vector.tensor_mul(out=even_cos[:], in0=even, in1=cos_all)
    nc.vector.tensor_mul(out=odd_sin[:], in0=odd, in1=sin_all)
    nc.vector.tensor_mul(out=even_sin[:], in0=even, in1=sin_all)
    nc.vector.tensor_mul(out=odd_cos[:], in0=odd, in1=cos_all)
    nc.vector.tensor_sub(out=even, in0=even_cos[:], in1=odd_sin[:])
    nc.vector.tensor_add(out=odd, in0=even_sin[:], in1=odd_cos[:])


def tile_diffucoderattention_pa_k_kernel(
    tc,
    hidden_states,
    Wq_words,
    Wq_scales,
    Wk_words,
    Wk_scales,
    Wv_words,
    Wv_scales,
    out_0,
    out_1,
    out_2,
):
    nc = tc.nc
    x_dram = hidden_states.rearrange("b s e -> (b s) e")

    with ExitStack() as ctx:
        keep = ctx.enter_context(tc.tile_pool(name="keep", bufs=1))
        x_pool = ctx.enter_context(tc.tile_pool(name="x_pool", bufs=PASSES // X_CHUNK_PASSES))
        stage = ctx.enter_context(tc.tile_pool(name="stage", bufs=3))
        weights = ctx.enter_context(tc.tile_pool(name="weights", bufs=WEIGHT_BUFS))
        work = ctx.enter_context(tc.tile_pool(name="work", bufs=1))
        sums = ctx.enter_context(tc.psum_pool(name="sums", bufs=1))
        flipped = ctx.enter_context(tc.psum_pool(name="flipped", bufs=2))

        q_planes = keep.tile([P, SLOTS, Q_COLS], U8, align_bytes=64)
        k_planes = keep.tile([P, SLOTS, KV_COLS], U8, align_bytes=64)
        v_planes = keep.tile([P, SLOTS, KV_COLS], U8, align_bytes=64)
        for planes in (q_planes, k_planes, v_planes):
            nc.vector.memset(planes[:].rearrange("p s n -> p (s n)").bitcast(I32), 0)

        identity = keep.tile([P, P], F32)
        make_identity(nc, identity[:])
        position_int = keep.tile([P, 1], I32)
        nc.gpsimd.iota(position_int[:], pattern=[[0, 1]], base=0, channel_multiplier=1)

        x_chunks = []
        for c in range(PASSES // X_CHUNK_PASSES):
            x_chunk = x_pool.tile([P, X_CHUNK_PASSES * K_PASS], BF16)
            nc.sync.dma_start(
                out=x_chunk[:],
                in_=x_dram[:, c * X_CHUNK_PASSES * K_PASS : (c + 1) * X_CHUNK_PASSES * K_PASS],
            )
            x_chunks.append(x_chunk)

        for slot in range(SLOTS):
            for quadrant in (0, 1):
                load_scale_rows(nc.sync, I32, q_planes, Wq_scales, slot, quadrant)
        load_upper_scales(nc, q_planes, Wq_scales)
        load_upper_scales(nc, k_planes, Wk_scales)
        load_upper_scales(nc, v_planes, Wv_scales)

        x_codes = keep.tile([P, PASSES, P], U32, align_bytes=64)
        x_scales = keep.tile([P, PASSES, P], U8, align_bytes=64)
        words_a_pass = K_PASS // 2
        for bank in range(PASSES // BANK_PASSES):
            first = bank * BANK_PASSES
            x_words = x_chunks[first // X_CHUNK_PASSES][:].bitcast(F32)
            turned = flipped.tile([P, BANK_PASSES, 2, P], F32)
            for i in range(BANK_PASSES):
                start_word = ((first + i) % X_CHUNK_PASSES) * words_a_pass
                for u in range(2):
                    nc.tensor.transpose(
                        turned[:, i, u, :],
                        x_words[:, start_word + u : start_word + words_a_pass : 2],
                        identity[:],
                    )
            grouped = stage.tile([P, BANK_PASSES * P * 4], BF16, align_bytes=64)
            grouped_words = grouped[:].bitcast(F32).rearrange(
                "p (i r u) -> p i r u", i=BANK_PASSES, u=2
            )
            if bank % 2 == 0:
                nc.vector.tensor_copy(out=grouped_words, in_=turned[:].rearrange("p i u r -> p i r u"))
            else:
                nc.scalar.copy(out=grouped_words, in_=turned[:].rearrange("p i u r -> p i r u"))
            nc.vector.quantize_mx(
                out=x_codes[:, first : first + BANK_PASSES, :]
                .rearrange("p i r -> p (i r)")
                .bitcast(FP8X4),
                scales=x_scales[:, first : first + BANK_PASSES, :].rearrange("p i r -> p (i r)"),
                in_=grouped[:],
            )

        position = keep.tile([P, 1], F32)
        nc.vector.tensor_copy(out=position[:], in_=position_int[:])
        phase = keep.tile([P, 2, PAIRS], F32)
        nc.vector.tensor_scalar_mul(out=phase[:, 0, 0:1], in0=position[:], scalar1=0.5 / math.pi)
        ratio = THETA ** (-2.0 / ROTATED)
        width = 1
        while width < PAIRS:
            nc.vector.tensor_scalar_mul(
                out=phase[:, 0, width : 2 * width], in0=phase[:, 0, 0:width], scalar1=ratio**width
            )
            width *= 2
        nc.vector.tensor_scalar_add(out=phase[:, 1, :], in0=phase[:, 0, :], scalar1=0.25)
        shifted = keep.tile([P, 2, PAIRS], F32)
        nc.vector.tensor_scalar_add(out=shifted[:], in0=phase[:], scalar1=ROUND_MAGIC)
        whole = keep.tile([P, 2, PAIRS], F32)
        nc.vector.tensor_scalar_sub(out=whole[:], in0=shifted[:], scalar1=ROUND_MAGIC)
        part = keep.tile([P, 2, PAIRS], F32)
        nc.vector.tensor_sub(out=part[:], in0=phase[:], in1=whole[:])
        sin_cos = keep.tile([P, 2, PAIRS], F32)
        nc.scalar.activation(out=sin_cos[:], in_=part[:], func=SIN, scale=2.0 * math.pi)
        sin = sin_cos[:, 0, :]
        cos = sin_cos[:, 1, :]

        q_tiles = Q_COLS // N_TILE
        q_sums = [sums.tile([P, N_TILE], F32, name="q_sum%d" % j) for j in range(q_tiles)]
        for g in range(PASSES):
            q_words = weights.tile([P, Q_COLS], U32, tag="weights", align_bytes=64)
            nc.sync.dma_start(
                out=q_words[:].bitcast(I32),
                in_=Wq_words[g].rearrange("p n t -> p (n t)").bitcast(I32),
            )
            planes, scales = ((k_planes, Wk_scales), (v_planes, Wv_scales))[g // 8]
            load_scale_rows(nc.sync, I32, planes, scales, (g % 8) // 2, g % 2)
            for j in range(q_tiles):
                cols = slice(j * N_TILE, (j + 1) * N_TILE)
                add_pass(nc, q_sums[j], x_codes, x_scales, g, q_words[:, cols], q_planes, cols)

        q_rows = keep.tile([P, Q_COLS], F32)
        for j in range(q_tiles):
            cols = slice(j * N_TILE, (j + 1) * N_TILE)
            if j % 2 == 0:
                nc.vector.tensor_copy(out=q_rows[:, cols], in_=q_sums[j][:])
            else:
                nc.scalar.copy(out=q_rows[:, cols], in_=q_sums[j][:])
        rotate_pairs(nc, work, q_rows[:], Q_COLS // HEAD, sin, cos)
        nc.scalar.dma_start(out=out_0.rearrange("b s h d -> (b s) (h d)"), in_=q_rows[:])

        k_sum = sums.tile([P, KV_COLS], F32, name="k_sum")
        for g, words in kv_passes(nc, weights, Wk_words, K_CHUNKS):
            add_pass(nc, k_sum, x_codes, x_scales, g, words, k_planes, slice(0, KV_COLS))
        k_rows = keep.tile([P, KV_COLS], F32)
        nc.scalar.copy(out=k_rows[:], in_=k_sum[:])
        rotate_pairs(nc, work, k_rows[:], KV_COLS // HEAD, sin, cos)
        nc.scalar.dma_start(out=out_1.rearrange("b s h d -> (b s) (h d)"), in_=k_rows[:])

        v_out = out_2.rearrange("b s h d -> (b s) (h d)")
        halves = (slice(0, KV_COLS // 2), slice(KV_COLS // 2, KV_COLS))
        v_sums = [flipped.tile([P, KV_COLS // 2], F32, name="v_sum%d" % j, tag="turned") for j in range(2)]
        for g, words in kv_passes(nc, weights, Wv_words, V_CHUNKS):
            for v_sum, cols in zip(v_sums, halves):
                add_pass(nc, v_sum, x_codes, x_scales, g, words[:, cols], v_planes, cols)
        v_left = keep.tile([P, KV_COLS // 2], F32)
        v_right = keep.tile([P, KV_COLS // 2], F32)
        nc.vector.tensor_copy(out=v_left[:], in_=v_sums[0][:])
        nc.scalar.copy(out=v_right[:], in_=v_sums[1][:])
        nc.sync.dma_start(out=v_out[:, halves[0]], in_=v_left[:])
        nc.scalar.dma_start(out=v_out[:, halves[1]], in_=v_right[:])
